import numpy as np
import ml_dtypes


BF16 = ml_dtypes.bfloat16


def bf(x):
    return np.asarray(x, np.float32).astype(BF16)


def f64(x):
    return np.asarray(x).astype(np.float64)


E2M1 = np.array([0.0, 0.5, 1.0, 1.5, 2.0, 3.0, 4.0, 6.0, -0.0, -0.5, -1.0, -1.5, -2.0, -3.0, -4.0, -6.0])


def pack_weight(w, fmt):
    k, n = w.shape
    w = f64(bf(w)).reshape(k // 32, 32, n)
    amax = np.abs(w).max(1)
    if fmt == "e4m3":
        byte = np.frexp(amax)[1] - 1 + 127 - 7
    else:
        mant, ex = np.frexp(amax / 6.0)
        byte = np.where(mant > 0.5, ex, ex - 1) + 127
    byte = np.clip(np.where(amax > 0, byte, 1), 1, 254)
    scaled = (w * np.exp2(127.0 - byte)[:, None, :]).reshape(k, n).astype(np.float32)
    by_word = np.ascontiguousarray(scaled.reshape(k // 512, 128, 4, n).transpose(0, 1, 3, 2))
    if fmt == "e4m3":
        words = by_word.astype(ml_dtypes.float8_e4m3fn).view(np.uint8)
    else:
        c = by_word.astype(ml_dtypes.float4_e2m1fn).view(np.uint8) & 0xF
        words = c[..., 0::2] | (c[..., 1::2] << 4)
    return np.ascontiguousarray(words), np.ascontiguousarray(byte.astype(np.uint8).reshape(k // 512, 16, n))


def unpack_weight(words, scales, fmt):
    g, p, n, _ = words.shape
    if fmt == "e4m3":
        vals = np.ascontiguousarray(words).view(ml_dtypes.float8_e4m3fn).astype(np.float64)
    else:
        nib = np.empty((g, p, n, 4), np.uint8)
        nib[..., 0::2] = words & 0xF
        nib[..., 1::2] = words >> 4
        vals = E2M1[nib]
    vals = vals * np.repeat(np.exp2(scales.astype(np.float64) - 127.0), 8, axis=1)[..., None]
    return vals.transpose(0, 1, 3, 2).reshape(g * 512, n)

def pack4(w):
    words, scales = pack_weight(w, "e2m1")
    return words.reshape(words.shape[0], 128, -1), scales


def unpack4(words, scales):
    return unpack_weight(words.reshape(words.shape[0], 128, -1, 2), scales, "e2m1")


def kspread(k):
    return np.exp2(np.repeat(np.random.randint(-6, 7, k // 32), 32).astype(np.float64))


B, T, D, H, HD = 2, 64, 8192, 8, 128
E = H * HD


def rope(u):
    inv_freq = 1.0 / (10000.0 ** (f64(np.arange(0, HD, 2)) / HD))
    pe = f64(np.arange(T))[:, None] * inv_freq[None, :]
    pe = np.repeat(pe, 2, axis=-1)
    u1 = u[..., 0::2]
    u2 = u[..., 1::2]
    rot = np.stack((-u2, u1), axis=-1).reshape(u.shape)
    return u * np.cos(pe) + rot * np.sin(pe)


def split_heads(u):
    return u.reshape(B, T, H, HD).transpose(0, 2, 1, 3)


def setup_inputs():
    s = kspread(D)
    x = np.random.standard_normal((B, T, D)) * s
    x_words, x_scales = pack4(np.ascontiguousarray(x.reshape(B * T, D).T))
    words, scales = pack4(np.random.standard_normal((D, 3 * E)) / np.sqrt(D) / s[:, None])
    return {"x_words": x_words, "x_scales": x_scales, "w_qkv_words": words, "w_qkv_scales": scales}


def reference(x_words, x_scales, w_qkv_words, w_qkv_scales):
    qkv = unpack4(x_words, x_scales).T.reshape(B, T, D) @ unpack4(w_qkv_words, w_qkv_scales)
    q, k, v = np.split(qkv, 3, axis=2)
    q, k, v = split_heads(q), split_heads(k), split_heads(v)
    return rope(q), rope(k), v

@@ -1,0 +1,192 @@
+import math
+from contextlib import ExitStack
+
+import concourse.mybir as mybir
+
+F32 = mybir.dt.float32
+I32 = mybir.dt.int32
+U8 = mybir.dt.uint8
+FP4X4 = mybir.dt.float4_e2m1fn_x4
+ALU = mybir.AluOpType
+ACT = mybir.ActivationFunctionType
+
+P = 128
+PASSES = 16
+TOKENS = 128
+BATCH = 2
+SEQ = 64
+HEADS = 8
+HD = 128
+PAIRS = HD // 2
+N_TILE = 512
+QK_COLS = 2048
+V_COLS = 1024
+ALL_COLS = QK_COLS + V_COLS
+RUN = 4
+QK_CHUNK = 2
+V_CHUNKS = (4, 4, 4, 2, 1, 1)
+
+FLOPS = 2 * TOKENS * 512 * PASSES * ALL_COLS
+
+
+def tile_selfattention_pa_kernel(tc, x_words, x_scales, w_qkv_words, w_qkv_scales, out_0, out_1, out_2):
+    nc = tc.nc
+    outs = (out_0, out_1, out_2)
+    with ExitStack() as ctx:
+        keep = ctx.enter_context(tc.tile_pool(name="keep", bufs=1))
+        work = ctx.enter_context(tc.tile_pool(name="work", bufs=2))
+        psum = ctx.enter_context(tc.psum_pool(name="psum", bufs=1))
+        ctx.enter_context(tc.manual_schedule())
+
+        xw = keep.tile([P, PASSES, 2 * TOKENS], U8, name="xw", align_bytes=64)
+        xs = keep.tile([P, PASSES, TOKENS], U8, name="xs", align_bytes=64)
+        ws = []
+        for k in range(PASSES // RUN):
+            ws_k = keep.tile([P, RUN, ALL_COLS], U8, name="ws%d" % k, align_bytes=64)
+            ws.append(ws_k)
+        wqk = []
+        for c in range(PASSES // QK_CHUNK):
+            wqk_c = keep.tile([P, QK_CHUNK, 2 * QK_COLS], U8, name="wqk%d" % c, align_bytes=64)
+            wqk.append(wqk_c)
+        wv = []
+        for c, n in enumerate(V_CHUNKS):
+            wv_c = keep.tile([P, n, 2 * V_COLS], U8, name="wv%d" % c, align_bytes=64)
+            wv.append(wv_c)
+
+        nc.vector.memset(xs[:].bitcast(I32), 0)
+        for k in range(PASSES // RUN):
+            nc.vector.memset(ws[k][:].bitcast(I32), 0)
+
+        def load_qk(c):
+            nc.sync.dma_start(
+                out=wqk[c][:].bitcast(I32),
+                in_=w_qkv_words[QK_CHUNK * c : QK_CHUNK * (c + 1), :, 0 : 2 * QK_COLS].rearrange("g p n -> p g n").bitcast(I32),
+            )
+
+        def load_w_scales(k):
+            for r in range(4):
+                nc.sync.dma_start(
+                    out=ws[k][r:P:32, :, :].bitcast(I32),
+                    in_=w_qkv_scales[RUN * k : RUN * (k + 1), r:16:4, :].rearrange("g q n -> q g n").bitcast(I32),
+                )
+
+        nc.sync.dma_start(out=xw[:].bitcast(I32), in_=x_words.rearrange("g p n -> p g n").bitcast(I32))
+        load_qk(0)
+        for r in range(4):
+            nc.sync.dma_start(
+                out=xs[r:P:32, :, :].bitcast(I32),
+                in_=x_scales[:, r:16:4, :].rearrange("g q n -> q g n").bitcast(I32),
+            )
+        load_w_scales(0)
+        load_qk(1)
+        for k in range(1, PASSES // RUN):
+            load_w_scales(k)
+            load_qk(2 * k)
+            load_qk(2 * k + 1)
+        g0 = 0
+        for c, n in enumerate(V_CHUNKS):
+            nc.sync.dma_start(
+                out=wv[c][:].bitcast(I32),
+                in_=w_qkv_words[g0 : g0 + n, :, 2 * QK_COLS : 2 * ALL_COLS].rearrange("g p n -> p g n").bitcast(I32),
+            )
+            g0 += n
+
+        pos = keep.tile([P, 1], F32, name="pos")
+        for b in range(BATCH):
+            nc.gpsimd.iota(pos[SEQ * b : SEQ * (b + 1), :], pattern=[[0, 1]], base=0, channel_multiplier=1,
+                           allow_small_or_imprecise_dtypes=True)
+        ratio = 10000.0 ** (-1.0 / PAIRS)
+        freq = keep.tile([P, PAIRS], F32, name="freq")
+        nc.vector.memset(freq[:, 0:1], 1.0)
+        for s in range(6):
+            w = 2 ** s
+            nc.vector.tensor_scalar(out=freq[:, w : 2 * w], in0=freq[:, 0:w], scalar1=ratio ** w, scalar2=None, op0=ALU.mult)
+        ang = keep.tile([P, 2 * PAIRS], F32, name="ang")
+        nc.vector.tensor_scalar(out=ang[:, 0:PAIRS], in0=freq[:], scalar1=pos[:, 0:1], scalar2=None, op0=ALU.mult)
+        nc.vector.tensor_scalar(out=ang[:, PAIRS : 2 * PAIRS], in0=freq[:], scalar1=pos[:, 0:1], scalar2=math.pi / 2,
+                                op0=ALU.mult, op1=ALU.add)
+        turns_i = keep.tile([P, 2 * PAIRS], I32, name="turns_i")
+        nc.vector.tensor_scalar(out=turns_i[:], in0=ang[:], scalar1=1.0 / (2.0 * math.pi), scalar2=None, op0=ALU.mult)
+        turns_f = keep.tile([P, 2 * PAIRS], F32, name="turns_f")
+        nc.vector.tensor_copy(out=turns_f[:], in_=turns_i[:])
+        red0 = keep.tile([P, 2 * PAIRS], F32, name="red0")
+        nc.vector.scalar_tensor_tensor(out=red0[:], in0=turns_f[:], scalar=-2.0 * math.pi, in1=ang[:], op0=ALU.mult, op1=ALU.add)
+        fix0 = keep.tile([P, 2 * PAIRS], F32, name="fix0")
+        nc.vector.tensor_scalar(out=fix0[:], in0=red0[:], scalar1=math.pi, scalar2=-2.0 * math.pi, op0=ALU.is_gt, op1=ALU.mult)
+        red1 = keep.tile([P, 2 * PAIRS], F32, name="red1")
+        nc.vector.tensor_tensor(out=red1[:], in0=red0[:], in1=fix0[:], op=ALU.add)
+        fix1 = keep.tile([P, 2 * PAIRS], F32, name="fix1")
+        nc.vector.tensor_scalar(out=fix1[:], in0=red1[:], scalar1=-math.pi, scalar2=2.0 * math.pi, op0=ALU.is_lt, op1=ALU.mult)
+        red2 = keep.tile([P, 2 * PAIRS], F32, name="red2")
+        nc.vector.tensor_tensor(out=red2[:], in0=red1[:], in1=fix1[:], op=ALU.add)
+        trig = keep.tile([P, 2 * PAIRS], F32, name="trig")
+        nc.scalar.activation(out=trig[:], in_=red2[:], func=ACT.Sin)
+        cos2 = keep.tile([P, PAIRS, 2], F32, name="cos2")
+        nc.vector.tensor_copy(out=cos2[:], in_=trig[:, PAIRS : 2 * PAIRS].unsqueeze(2).to_broadcast([P, PAIRS, 2]))
+        nsin = keep.tile([P, PAIRS], F32, name="nsin")
+        nc.vector.tensor_scalar(out=nsin[:], in0=trig[:, 0:PAIRS], scalar1=-1.0, scalar2=None, op0=ALU.mult)
+
+        HB = N_TILE // HD
+        cos_b = cos2[:].rearrange("p i e -> p (i e)").unsqueeze(1).to_broadcast([P, HB, HD])
+        sin_b = trig[:, 0:PAIRS].unsqueeze(1).to_broadcast([P, HB, PAIRS])
+        nsin_b = nsin[:].unsqueeze(1).to_broadcast([P, HB, PAIRS])
+
+        acc = []
+        for j in range(ALL_COLS // N_TILE):
+            acc_j = psum.tile([P, N_TILE], F32, name="acc%d" % j)
+            acc.append(acc_j)
+
+        def mm(j, g, codes):
+            nc.tensor.matmul_mx(
+                out=acc[j][:],
+                lhsT=xw[:, g, :].bitcast(FP4X4),
+                lhsT_scale=xs[:, g, :],
+                rhs=codes.bitcast(FP4X4),
+                rhs_scale=ws[g // RUN][:, g % RUN, N_TILE * j : N_TILE * (j + 1)],
+                start=(g == 0),
+                stop=(g == PASSES - 1),
+            )
+
+        for g in range(PASSES):
+            for j in range(QK_COLS // N_TILE):
+                mm(j, g, wqk[g // QK_CHUNK][:, g % QK_CHUNK, 2 * N_TILE * j : 2 * N_TILE * (j + 1)])
+
+        res = []
+        for t in range(3):
+            res_t = keep.tile([P, HEADS * HD], F32, name="res%d" % t)
+            res.append(res_t)
+
+        def store(eng, t, b):
+            eng.dma_start(
+                out=outs[t][b].rearrange("h s d -> s h d"),
+                in_=res[t][SEQ * b : SEQ * (b + 1), :].rearrange("p (h d) -> p h d", h=HEADS),
+            )
+
+        for j in range(QK_COLS // N_TILE):
+            u = acc[j][:].rearrange("p (h i e) -> p h i e", h=HB, e=2)
+            cross = work.tile([P, 2, HB, PAIRS], F32, name="cross")
+            nc.vector.tensor_tensor(out=cross[:, 0], in0=u[:, :, :, 1], in1=nsin_b, op=ALU.mult)
+            nc.vector.tensor_tensor(out=cross[:, 1], in0=u[:, :, :, 0], in1=sin_b, op=ALU.mult)
+            direct = work.tile([P, HB, HD], F32, name="direct")
+            nc.vector.tensor_tensor(out=direct[:], in0=acc[j][:].rearrange("p (h d) -> p h d", h=HB), in1=cos_b, op=ALU.mult)
+            half = N_TILE * (j % 2)
+            nc.gpsimd.tensor_tensor(
+                out=res[j // 2][:, half : half + N_TILE].rearrange("p (h i e) -> p h i e", h=HB, e=2),
+                in0=direct[:].rearrange("p h (i e) -> p h i e", e=2),
+                in1=cross[:].rearrange("p e h i -> p h i e"),
+                op=ALU.add,
+            )
+            if j % 2 == 1:
+                store(nc.scalar, j // 2, 0)
+                store(nc.scalar, j // 2, 1)
+
+        g = 0
+        for c, n in enumerate(V_CHUNKS):
+            for i in range(n):
+                for j in range(V_COLS // N_TILE):
+                    mm(QK_COLS // N_TILE + j, g, wv[c][:, i, 2 * N_TILE * j : 2 * N_TILE * (j + 1)])
+                g += 1
+        nc.scalar.copy(out=res[2][:, 0:N_TILE], in_=acc[4][:])
+        nc.vector.tensor_copy(out=res[2][:, N_TILE : 2 * N_TILE], in_=acc[5][:])
+        store(nc.sync, 2, 0)
+        store(nc.scalar, 2, 1)

@@ -22,8 +22,8 @@ N_TILE = 512
 QK_COLS = 2048
 V_COLS = 1024
 ALL_COLS = QK_COLS + V_COLS
-RUN = 4
-QK_CHUNK = 2
+RUN = 2
+QK_CHUNKS = (1, 1, 2, 2, 2, 2, 2, 2, 2)
 V_CHUNKS = (4, 4, 4, 2, 1, 1)
 
 FLOPS = 2 * TOKENS * 512 * PASSES * ALL_COLS
@@ -45,8 +45,8 @@ def tile_selfattention_pa_kernel(tc, x_words, x_scales, w_qkv_words, w_qkv_scale
             ws_k = keep.tile([P, RUN, ALL_COLS], U8, name="ws%d" % k, align_bytes=64)
             ws.append(ws_k)
         wqk = []
-        for c in range(PASSES // QK_CHUNK):
-            wqk_c = keep.tile([P, QK_CHUNK, 2 * QK_COLS], U8, name="wqk%d" % c, align_bytes=64)
+        for c, n in enumerate(QK_CHUNKS):
+            wqk_c = keep.tile([P, n, 2 * QK_COLS], U8, name="wqk%d" % c, align_bytes=64)
             wqk.append(wqk_c)
         wv = []
         for c, n in enumerate(V_CHUNKS):
@@ -57,12 +57,6 @@ def tile_selfattention_pa_kernel(tc, x_words, x_scales, w_qkv_words, w_qkv_scale
         for k in range(PASSES // RUN):
             nc.vector.memset(ws[k][:].bitcast(I32), 0)
 
-        def load_qk(c):
-            nc.sync.dma_start(
-                out=wqk[c][:].bitcast(I32),
-                in_=w_qkv_words[QK_CHUNK * c : QK_CHUNK * (c + 1), :, 0 : 2 * QK_COLS].rearrange("g p n -> p g n").bitcast(I32),
-            )
-
         def load_w_scales(k):
             for r in range(4):
                 nc.sync.dma_start(
@@ -70,26 +64,25 @@ def tile_selfattention_pa_kernel(tc, x_words, x_scales, w_qkv_words, w_qkv_scale
                     in_=w_qkv_scales[RUN * k : RUN * (k + 1), r:16:4, :].rearrange("g q n -> q g n").bitcast(I32),
                 )
 
+        def load_codes(tiles, chunks, col0, col1):
+            g0 = 0
+            for c, n in enumerate(chunks):
+                nc.sync.dma_start(
+                    out=tiles[c][:].bitcast(I32),
+                    in_=w_qkv_words[g0 : g0 + n, :, col0:col1].rearrange("g p n -> p g n").bitcast(I32),
+                )
+                g0 += n
+
         nc.sync.dma_start(out=xw[:].bitcast(I32), in_=x_words.rearrange("g p n -> p g n").bitcast(I32))
-        load_qk(0)
         for r in range(4):
             nc.sync.dma_start(
                 out=xs[r:P:32, :, :].bitcast(I32),
                 in_=x_scales[:, r:16:4, :].rearrange("g q n -> q g n").bitcast(I32),
             )
-        load_w_scales(0)
-        load_qk(1)
-        for k in range(1, PASSES // RUN):
+        for k in range(PASSES // RUN):
             load_w_scales(k)
-            load_qk(2 * k)
-            load_qk(2 * k + 1)
-        g0 = 0
-        for c, n in enumerate(V_CHUNKS):
-            nc.sync.dma_start(
-                out=wv[c][:].bitcast(I32),
-                in_=w_qkv_words[g0 : g0 + n, :, 2 * QK_COLS : 2 * ALL_COLS].rearrange("g p n -> p g n").bitcast(I32),
-            )
-            g0 += n
+        load_codes(wqk, QK_CHUNKS, 0, 2 * QK_COLS)
+        load_codes(wv, V_CHUNKS, 2 * QK_COLS, 2 * ALL_COLS)
 
         pos = keep.tile([P, 1], F32, name="pos")
         for b in range(BATCH):
@@ -147,9 +140,12 @@ def tile_selfattention_pa_kernel(tc, x_words, x_scales, w_qkv_words, w_qkv_scale
                 stop=(g == PASSES - 1),
             )
 
-        for g in range(PASSES):
-            for j in range(QK_COLS // N_TILE):
-                mm(j, g, wqk[g // QK_CHUNK][:, g % QK_CHUNK, 2 * N_TILE * j : 2 * N_TILE * (j + 1)])
+        g = 0
+        for c, n in enumerate(QK_CHUNKS):
+            for i in range(n):
+                for j in range(QK_COLS // N_TILE):
+                    mm(j, g, wqk[c][:, i, 2 * N_TILE * j : 2 * N_TILE * (j + 1)])
+                g += 1
 
         res = []
         for t in range(3):
@@ -178,7 +174,7 @@ def tile_selfattention_pa_kernel(tc, x_words, x_scales, w_qkv_words, w_qkv_scale
             )
             if j % 2 == 1:
                 store(nc.scalar, j // 2, 0)
-                store(nc.scalar, j // 2, 1)
+                store(nc.gpsimd, j // 2, 1)
 
         g = 0
         for c, n in enumerate(V_CHUNKS):

@@ -22,7 +22,7 @@ N_TILE = 512
 QK_COLS = 2048
 V_COLS = 1024
 ALL_COLS = QK_COLS + V_COLS
-RUN = 2
+SCALE_GROUPS = (4, 4, 8)
 QK_CHUNKS = (1, 1, 2, 2, 2, 2, 2, 2, 2)
 V_CHUNKS = (4, 4, 4, 2, 1, 1)
 
@@ -41,9 +41,12 @@ def tile_selfattention_pa_kernel(tc, x_words, x_scales, w_qkv_words, w_qkv_scale
         xw = keep.tile([P, PASSES, 2 * TOKENS], U8, name="xw", align_bytes=64)
         xs = keep.tile([P, PASSES, TOKENS], U8, name="xs", align_bytes=64)
         ws = []
-        for k in range(PASSES // RUN):
-            ws_k = keep.tile([P, RUN, ALL_COLS], U8, name="ws%d" % k, align_bytes=64)
+        ws_of_pass = []
+        for k, n in enumerate(SCALE_GROUPS):
+            ws_k = keep.tile([P, n, ALL_COLS], U8, name="ws%d" % k, align_bytes=64)
             ws.append(ws_k)
+            for i in range(n):
+                ws_of_pass.append((k, i))
         wqk = []
         for c, n in enumerate(QK_CHUNKS):
             wqk_c = keep.tile([P, n, 2 * QK_COLS], U8, name="wqk%d" % c, align_bytes=64)
@@ -54,14 +57,15 @@ def tile_selfattention_pa_kernel(tc, x_words, x_scales, w_qkv_words, w_qkv_scale
             wv.append(wv_c)
 
         nc.vector.memset(xs[:].bitcast(I32), 0)
-        for k in range(PASSES // RUN):
+        for k in range(len(SCALE_GROUPS)):
             nc.vector.memset(ws[k][:].bitcast(I32), 0)
 
-        def load_w_scales(k):
-            for r in range(4):
+        def load_scales(plane, rows):
+            for q0 in range(8):
+                p0 = 32 * (q0 // 4) + q0 % 4
                 nc.sync.dma_start(
-                    out=ws[k][r:P:32, :, :].bitcast(I32),
-                    in_=w_qkv_scales[RUN * k : RUN * (k + 1), r:16:4, :].rearrange("g q n -> q g n").bitcast(I32),
+                    out=plane[p0:P:64, :, :].bitcast(I32),
+                    in_=rows[:, q0:16:8, :].rearrange("g q n -> q g n").bitcast(I32),
                 )
 
         def load_codes(tiles, chunks, col0, col1):
@@ -74,13 +78,15 @@ def tile_selfattention_pa_kernel(tc, x_words, x_scales, w_qkv_words, w_qkv_scale
                 g0 += n
 
         nc.sync.dma_start(out=xw[:].bitcast(I32), in_=x_words.rearrange("g p n -> p g n").bitcast(I32))
+        g0 = 0
+        for k, n in enumerate(SCALE_GROUPS):
+            load_scales(ws[k], w_qkv_scales[g0 : g0 + n])
+            g0 += n
         for r in range(4):
             nc.sync.dma_start(
                 out=xs[r:P:32, :, :].bitcast(I32),
                 in_=x_scales[:, r:16:4, :].rearrange("g q n -> q g n").bitcast(I32),
             )
-        for k in range(PASSES // RUN):
-            load_w_scales(k)
         load_codes(wqk, QK_CHUNKS, 0, 2 * QK_COLS)
         load_codes(wv, V_CHUNKS, 2 * QK_COLS, 2 * ALL_COLS)
 
@@ -135,7 +141,7 @@ def tile_selfattention_pa_kernel(tc, x_words, x_scales, w_qkv_words, w_qkv_scale
                 lhsT=xw[:, g, :].bitcast(FP4X4),
                 lhsT_scale=xs[:, g, :],
                 rhs=codes.bitcast(FP4X4),
-                rhs_scale=ws[g // RUN][:, g % RUN, N_TILE * j : N_TILE * (j + 1)],
+                rhs_scale=ws[ws_of_pass[g][0]][:, ws_of_pass[g][1], N_TILE * j : N_TILE * (j + 1)],
                 start=(g == 0),
                 stop=(g == PASSES - 1),
             )

@@ -19,12 +19,19 @@ HEADS = 8
 HD = 128
 PAIRS = HD // 2
 N_TILE = 512
-QK_COLS = 2048
-V_COLS = 1024
-ALL_COLS = QK_COLS + V_COLS
+BANKS = 6
+QK_BANKS = 4
+HB = N_TILE // HD
+ALL_COLS = BANKS * N_TILE
 SCALE_GROUPS = (4, 4, 8)
-QK_CHUNKS = (1, 1, 2, 2, 2, 2, 2, 2, 2)
-V_CHUNKS = (4, 4, 4, 2, 1, 1)
+
+QK_LOADS = (
+    (0, 1, 0, 4), (1, 1, 0, 4), (2, 2, 0, 4), (4, 2, 0, 4), (6, 2, 0, 4),
+    (8, 2, 0, 4), (10, 2, 0, 4), (12, 2, 0, 4), (14, 1, 0, 4), (15, 1, 0, 4),
+)
+V0_LOADS = ((0, 4, 4, 6), (4, 4, 4, 6), (8, 4, 4, 6), (12, 4, 4, 5))
+V1_LOADS = ((12, 2, 5, 6), (14, 1, 5, 6), (15, 1, 5, 6))
+SHIFT = 32
 
 FLOPS = 2 * TOKENS * 512 * PASSES * ALL_COLS
 
@@ -34,10 +41,12 @@ def tile_selfattention_pa_kernel(tc, x_words, x_scales, w_qkv_words, w_qkv_scale
     outs = (out_0, out_1, out_2)
     with ExitStack() as ctx:
         keep = ctx.enter_context(tc.tile_pool(name="keep", bufs=1))
-        work = ctx.enter_context(tc.tile_pool(name="work", bufs=2))
+        work = ctx.enter_context(tc.tile_pool(name="work", bufs=4))
         psum = ctx.enter_context(tc.psum_pool(name="psum", bufs=1))
         ctx.enter_context(tc.manual_schedule())
 
+        xw_in = keep.tile([P, PASSES, 2 * TOKENS], U8, name="xw_in", align_bytes=64)
+        xs_in = keep.tile([P, PASSES, TOKENS], U8, name="xs_in", align_bytes=64)
         xw = keep.tile([P, PASSES, 2 * TOKENS], U8, name="xw", align_bytes=64)
         xs = keep.tile([P, PASSES, TOKENS], U8, name="xs", align_bytes=64)
         ws = []
@@ -46,53 +55,49 @@ def tile_selfattention_pa_kernel(tc, x_words, x_scales, w_qkv_words, w_qkv_scale
             ws_k = keep.tile([P, n, ALL_COLS], U8, name="ws%d" % k, align_bytes=64)
             ws.append(ws_k)
             for i in range(n):
-                ws_of_pass.append((k, i))
-        wqk = []
-        for c, n in enumerate(QK_CHUNKS):
-            wqk_c = keep.tile([P, n, 2 * QK_COLS], U8, name="wqk%d" % c, align_bytes=64)
-            wqk.append(wqk_c)
-        wv = []
-        for c, n in enumerate(V_CHUNKS):
-            wv_c = keep.tile([P, n, 2 * V_COLS], U8, name="wv%d" % c, align_bytes=64)
-            wv.append(wv_c)
+                ws_of_pass.append(ws_k[:, i, :])
 
-        nc.vector.memset(xs[:].bitcast(I32), 0)
-        for k in range(len(SCALE_GROUPS)):
-            nc.vector.memset(ws[k][:].bitcast(I32), 0)
+        nc.vector.memset(xs_in[:].bitcast(I32), 0)
+        for ws_k in ws:
+            nc.vector.memset(ws_k[:].bitcast(I32), 0)
 
-        def load_scales(plane, rows):
+        nc.sync.dma_start(out=xw_in[:].bitcast(I32), in_=x_words.rearrange("g p n -> p g n").bitcast(I32))
+        g0 = 0
+        for k, n in enumerate(SCALE_GROUPS):
             for q0 in range(8):
                 p0 = 32 * (q0 // 4) + q0 % 4
                 nc.sync.dma_start(
-                    out=plane[p0:P:64, :, :].bitcast(I32),
-                    in_=rows[:, q0:16:8, :].rearrange("g q n -> q g n").bitcast(I32),
+                    out=ws[k][p0:P:64, :, :].bitcast(I32),
+                    in_=w_qkv_scales[g0 : g0 + n, q0:16:8, :].rearrange("g q n -> q g n").bitcast(I32),
                 )
-
-        def load_codes(tiles, chunks, col0, col1):
-            g0 = 0
-            for c, n in enumerate(chunks):
-                nc.sync.dma_start(
-                    out=tiles[c][:].bitcast(I32),
-                    in_=w_qkv_words[g0 : g0 + n, :, col0:col1].rearrange("g p n -> p g n").bitcast(I32),
-                )
-                g0 += n
-
-        nc.sync.dma_start(out=xw[:].bitcast(I32), in_=x_words.rearrange("g p n -> p g n").bitcast(I32))
-        g0 = 0
-        for k, n in enumerate(SCALE_GROUPS):
-            load_scales(ws[k], w_qkv_scales[g0 : g0 + n])
             g0 += n
-        for r in range(4):
+            if k == 0:
+                for r in range(4):
+                    nc.sync.dma_start(
+                        out=xs_in[r:P:32, :, :].bitcast(I32),
+                        in_=x_scales[:, r:16:4, :].rearrange("g q n -> q g n").bitcast(I32),
+                    )
+        codes = {}
+        for first, n, j0, j1 in QK_LOADS + V0_LOADS + V1_LOADS:
+            w_t = keep.tile([P, n, 2 * N_TILE * (j1 - j0)], U8, name="w%d_%d" % (first, j0), align_bytes=64)
             nc.sync.dma_start(
-                out=xs[r:P:32, :, :].bitcast(I32),
-                in_=x_scales[:, r:16:4, :].rearrange("g q n -> q g n").bitcast(I32),
+                out=w_t[:].bitcast(I32),
+                in_=w_qkv_words[first : first + n, :, 2 * N_TILE * j0 : 2 * N_TILE * j1].rearrange("g p n -> p g n").bitcast(I32),
             )
-        load_codes(wqk, QK_CHUNKS, 0, 2 * QK_COLS)
-        load_codes(wv, V_CHUNKS, 2 * QK_COLS, 2 * ALL_COLS)
+            for i in range(n):
+                for j in range(j0, j1):
+                    codes[(first + i, j)] = w_t[:, i, 2 * N_TILE * (j - j0) : 2 * N_TILE * (j - j0 + 1)]
+
+        def rotate(dst, src, width):
+            cut = width * (TOKENS - SHIFT)
+            nc.vector.tensor_copy(out=dst[:, :, width * SHIFT :].bitcast(I32), in_=src[:, :, 0:cut].bitcast(I32))
+            nc.vector.tensor_copy(out=dst[:, :, 0 : width * SHIFT].bitcast(I32), in_=src[:, :, cut:].bitcast(I32))
+
+        rotate(xw, xw_in, 2)
 
         pos = keep.tile([P, 1], F32, name="pos")
-        for b in range(BATCH):
-            nc.gpsimd.iota(pos[SEQ * b : SEQ * (b + 1), :], pattern=[[0, 1]], base=0, channel_multiplier=1,
+        for quad in range(4):
+            nc.gpsimd.iota(pos[32 * quad : 32 * (quad + 1), :], pattern=[[0, 1]], base=(32 * quad - SHIFT) % SEQ, channel_multiplier=1,
                            allow_small_or_imprecise_dtypes=True)
         ratio = 10000.0 ** (-1.0 / PAIRS)
         freq = keep.tile([P, PAIRS], F32, name="freq")
@@ -124,71 +129,83 @@ def tile_selfattention_pa_kernel(tc, x_words, x_scales, w_qkv_words, w_qkv_scale
         nc.vector.tensor_copy(out=cos2[:], in_=trig[:, PAIRS : 2 * PAIRS].unsqueeze(2).to_broadcast([P, PAIRS, 2]))
         nsin = keep.tile([P, PAIRS], F32, name="nsin")
         nc.vector.tensor_scalar(out=nsin[:], in0=trig[:, 0:PAIRS], scalar1=-1.0, scalar2=None, op0=ALU.mult)
-
-        HB = N_TILE // HD
         cos_b = cos2[:].rearrange("p i e -> p (i e)").unsqueeze(1).to_broadcast([P, HB, HD])
         sin_b = trig[:, 0:PAIRS].unsqueeze(1).to_broadcast([P, HB, PAIRS])
         nsin_b = nsin[:].unsqueeze(1).to_broadcast([P, HB, PAIRS])
+        rotate(xs, xs_in, 1)
 
         acc = []
-        for j in range(ALL_COLS // N_TILE):
+        for j in range(BANKS):
             acc_j = psum.tile([P, N_TILE], F32, name="acc%d" % j)
             acc.append(acc_j)
 
-        def mm(j, g, codes):
-            nc.tensor.matmul_mx(
-                out=acc[j][:],
-                lhsT=xw[:, g, :].bitcast(FP4X4),
-                lhsT_scale=xs[:, g, :],
-                rhs=codes.bitcast(FP4X4),
-                rhs_scale=ws[ws_of_pass[g][0]][:, ws_of_pass[g][1], N_TILE * j : N_TILE * (j + 1)],
-                start=(g == 0),
-                stop=(g == PASSES - 1),
-            )
-
-        g = 0
-        for c, n in enumerate(QK_CHUNKS):
-            for i in range(n):
-                for j in range(QK_COLS // N_TILE):
-                    mm(j, g, wqk[c][:, i, 2 * N_TILE * j : 2 * N_TILE * (j + 1)])
-                g += 1
+        def multiply(loads):
+            for first, n, j0, j1 in loads:
+                for g in range(first, first + n):
+                    for j in range(j0, j1):
+                        nc.tensor.matmul_mx(
+                            out=acc[j][:],
+                            lhsT=xw[:, g, :].bitcast(FP4X4),
+                            lhsT_scale=xs[:, g, :],
+                            rhs=codes[(g, j)].bitcast(FP4X4),
+                            rhs_scale=ws_of_pass[g][:, N_TILE * j : N_TILE * (j + 1)],
+                            start=(g == 0),
+                            stop=(g == PASSES - 1),
+                        )
 
         res = []
         for t in range(3):
             res_t = keep.tile([P, HEADS * HD], F32, name="res%d" % t)
             res.append(res_t)
 
-        def store(eng, t, b):
+        def store(eng, t, n0, n1, h0, h1):
+            b = n0 // SEQ
+            p0 = (n0 + SHIFT) % TOKENS
             eng.dma_start(
-                out=outs[t][b].rearrange("h s d -> s h d"),
-                in_=res[t][SEQ * b : SEQ * (b + 1), :].rearrange("p (h d) -> p h d", h=HEADS),
+                out=outs[t][b, h0:h1, n0 - SEQ * b : n1 - SEQ * b, :].rearrange("h s d -> s h d"),
+                in_=res[t][p0 : p0 + n1 - n0, HD * h0 : HD * h1].rearrange("p (h d) -> p h d", d=HD),
             )
 
-        for j in range(QK_COLS // N_TILE):
+        def rope_products(j):
             u = acc[j][:].rearrange("p (h i e) -> p h i e", h=HB, e=2)
             cross = work.tile([P, 2, HB, PAIRS], F32, name="cross")
             nc.vector.tensor_tensor(out=cross[:, 0], in0=u[:, :, :, 1], in1=nsin_b, op=ALU.mult)
             nc.vector.tensor_tensor(out=cross[:, 1], in0=u[:, :, :, 0], in1=sin_b, op=ALU.mult)
             direct = work.tile([P, HB, HD], F32, name="direct")
             nc.vector.tensor_tensor(out=direct[:], in0=acc[j][:].rearrange("p (h d) -> p h d", h=HB), in1=cos_b, op=ALU.mult)
+            return direct, cross
+
+        def rope_sum(eng, j, direct, cross):
             half = N_TILE * (j % 2)
-            nc.gpsimd.tensor_tensor(
+            eng.tensor_tensor(
                 out=res[j // 2][:, half : half + N_TILE].rearrange("p (h i e) -> p h i e", h=HB, e=2),
                 in0=direct[:].rearrange("p h (i e) -> p h i e", e=2),
                 in1=cross[:].rearrange("p e h i -> p h i e"),
                 op=ALU.add,
             )
-            if j % 2 == 1:
-                store(nc.scalar, j // 2, 0)
-                store(nc.gpsimd, j // 2, 1)
 
-        g = 0
-        for c, n in enumerate(V_CHUNKS):
-            for i in range(n):
-                for j in range(V_COLS // N_TILE):
-                    mm(QK_COLS // N_TILE + j, g, wv[c][:, i, 2 * N_TILE * j : 2 * N_TILE * (j + 1)])
-                g += 1
+        multiply(QK_LOADS)
+        for j in (0, 1):
+            direct, cross = rope_products(j)
+            rope_sum(nc.gpsimd, j, direct, cross)
+        store(nc.scalar, 0, 0, 64, 0, HEADS)
+        store(nc.gpsimd, 0, 64, 96, 0, HEADS)
+        store(nc.gpsimd, 0, 96, 128, 0, HEADS)
+        parts = []
+        for j in (2, 3):
+            parts.append(rope_products(j))
+        for j in (2, 3):
+            rope_sum(nc.vector, j, parts[j - 2][0], parts[j - 2][1])
+        store(nc.scalar, 1, 0, 64, 0, HEADS)
+        store(nc.sync, 1, 64, 96, 0, HEADS)
+        store(nc.sync, 1, 96, 128, 0, HEADS)
+        multiply(V0_LOADS)
         nc.scalar.copy(out=res[2][:, 0:N_TILE], in_=acc[4][:])
+        store(nc.scalar, 2, 0, 64, 0, HB)
+        store(nc.gpsimd, 2, 64, 96, 0, HB)
+        store(nc.gpsimd, 2, 96, 128, 0, HB)
+        multiply(V1_LOADS)
         nc.vector.tensor_copy(out=res[2][:, N_TILE : 2 * N_TILE], in_=acc[5][:])
-        store(nc.sync, 2, 0)
-        store(nc.scalar, 2, 1)
+        store(nc.sync, 2, 0, 64, HB, HEADS)
+        store(nc.scalar, 2, 64, 96, HB, HEADS)
+        store(nc.scalar, 2, 96, 128, HB, HEADS)

@@ -19,19 +19,12 @@ HEADS = 8
 HD = 128
 PAIRS = HD // 2
 N_TILE = 512
-BANKS = 6
-QK_BANKS = 4
-HB = N_TILE // HD
-ALL_COLS = BANKS * N_TILE
+QK_COLS = 2048
+V_COLS = 1024
+ALL_COLS = QK_COLS + V_COLS
 SCALE_GROUPS = (4, 4, 8)
-
-QK_LOADS = (
-    (0, 1, 0, 4), (1, 1, 0, 4), (2, 2, 0, 4), (4, 2, 0, 4), (6, 2, 0, 4),
-    (8, 2, 0, 4), (10, 2, 0, 4), (12, 2, 0, 4), (14, 1, 0, 4), (15, 1, 0, 4),
-)
-V0_LOADS = ((0, 4, 4, 6), (4, 4, 4, 6), (8, 4, 4, 6), (12, 4, 4, 5))
-V1_LOADS = ((12, 2, 5, 6), (14, 1, 5, 6), (15, 1, 5, 6))
-SHIFT = 32
+QK_CHUNKS = (1, 1, 2, 2, 2, 2, 2, 2, 2)
+V_CHUNKS = (4, 4, 4, 2, 1, 1)
 
 FLOPS = 2 * TOKENS * 512 * PASSES * ALL_COLS
 
@@ -41,12 +34,10 @@ def tile_selfattention_pa_kernel(tc, x_words, x_scales, w_qkv_words, w_qkv_scale
     outs = (out_0, out_1, out_2)
     with ExitStack() as ctx:
         keep = ctx.enter_context(tc.tile_pool(name="keep", bufs=1))
-        work = ctx.enter_context(tc.tile_pool(name="work", bufs=4))
+        work = ctx.enter_context(tc.tile_pool(name="work", bufs=2))
         psum = ctx.enter_context(tc.psum_pool(name="psum", bufs=1))
         ctx.enter_context(tc.manual_schedule())
 
-        xw_in = keep.tile([P, PASSES, 2 * TOKENS], U8, name="xw_in", align_bytes=64)
-        xs_in = keep.tile([P, PASSES, TOKENS], U8, name="xs_in", align_bytes=64)
         xw = keep.tile([P, PASSES, 2 * TOKENS], U8, name="xw", align_bytes=64)
         xs = keep.tile([P, PASSES, TOKENS], U8, name="xs", align_bytes=64)
         ws = []
@@ -55,49 +46,53 @@ def tile_selfattention_pa_kernel(tc, x_words, x_scales, w_qkv_words, w_qkv_scale
             ws_k = keep.tile([P, n, ALL_COLS], U8, name="ws%d" % k, align_bytes=64)
             ws.append(ws_k)
             for i in range(n):
-                ws_of_pass.append(ws_k[:, i, :])
+                ws_of_pass.append((k, i))
+        wqk = []
+        for c, n in enumerate(QK_CHUNKS):
+            wqk_c = keep.tile([P, n, 2 * QK_COLS], U8, name="wqk%d" % c, align_bytes=64)
+            wqk.append(wqk_c)
+        wv = []
+        for c, n in enumerate(V_CHUNKS):
+            wv_c = keep.tile([P, n, 2 * V_COLS], U8, name="wv%d" % c, align_bytes=64)
+            wv.append(wv_c)
 
-        nc.vector.memset(xs_in[:].bitcast(I32), 0)
-        for ws_k in ws:
-            nc.vector.memset(ws_k[:].bitcast(I32), 0)
+        nc.vector.memset(xs[:].bitcast(I32), 0)
+        for k in range(len(SCALE_GROUPS)):
+            nc.vector.memset(ws[k][:].bitcast(I32), 0)
 
-        nc.sync.dma_start(out=xw_in[:].bitcast(I32), in_=x_words.rearrange("g p n -> p g n").bitcast(I32))
-        g0 = 0
-        for k, n in enumerate(SCALE_GROUPS):
+        def load_scales(plane, rows):
             for q0 in range(8):
                 p0 = 32 * (q0 // 4) + q0 % 4
                 nc.sync.dma_start(
-                    out=ws[k][p0:P:64, :, :].bitcast(I32),
-                    in_=w_qkv_scales[g0 : g0 + n, q0:16:8, :].rearrange("g q n -> q g n").bitcast(I32),
+                    out=plane[p0:P:64, :, :].bitcast(I32),
+                    in_=rows[:, q0:16:8, :].rearrange("g q n -> q g n").bitcast(I32),
                 )
+
+        def load_codes(tiles, chunks, col0, col1):
+            g0 = 0
+            for c, n in enumerate(chunks):
+                nc.sync.dma_start(
+                    out=tiles[c][:].bitcast(I32),
+                    in_=w_qkv_words[g0 : g0 + n, :, col0:col1].rearrange("g p n -> p g n").bitcast(I32),
+                )
+                g0 += n
+
+        nc.sync.dma_start(out=xw[:].bitcast(I32), in_=x_words.rearrange("g p n -> p g n").bitcast(I32))
+        g0 = 0
+        for k, n in enumerate(SCALE_GROUPS):
+            load_scales(ws[k], w_qkv_scales[g0 : g0 + n])
             g0 += n
-            if k == 0:
-                for r in range(4):
-                    nc.sync.dma_start(
-                        out=xs_in[r:P:32, :, :].bitcast(I32),
-                        in_=x_scales[:, r:16:4, :].rearrange("g q n -> q g n").bitcast(I32),
-                    )
-        codes = {}
-        for first, n, j0, j1 in QK_LOADS + V0_LOADS + V1_LOADS:
-            w_t = keep.tile([P, n, 2 * N_TILE * (j1 - j0)], U8, name="w%d_%d" % (first, j0), align_bytes=64)
+        for r in range(4):
             nc.sync.dma_start(
-                out=w_t[:].bitcast(I32),
-                in_=w_qkv_words[first : first + n, :, 2 * N_TILE * j0 : 2 * N_TILE * j1].rearrange("g p n -> p g n").bitcast(I32),
+                out=xs[r:P:32, :, :].bitcast(I32),
+                in_=x_scales[:, r:16:4, :].rearrange("g q n -> q g n").bitcast(I32),
             )
-            for i in range(n):
-                for j in range(j0, j1):
-                    codes[(first + i, j)] = w_t[:, i, 2 * N_TILE * (j - j0) : 2 * N_TILE * (j - j0 + 1)]
-
-        def rotate(dst, src, width):
-            cut = width * (TOKENS - SHIFT)
-            nc.vector.tensor_copy(out=dst[:, :, width * SHIFT :].bitcast(I32), in_=src[:, :, 0:cut].bitcast(I32))
-            nc.vector.tensor_copy(out=dst[:, :, 0 : width * SHIFT].bitcast(I32), in_=src[:, :, cut:].bitcast(I32))
-
-        rotate(xw, xw_in, 2)
+        load_codes(wqk, QK_CHUNKS, 0, 2 * QK_COLS)
+        load_codes(wv, V_CHUNKS, 2 * QK_COLS, 2 * ALL_COLS)
 
         pos = keep.tile([P, 1], F32, name="pos")
-        for quad in range(4):
-            nc.gpsimd.iota(pos[32 * quad : 32 * (quad + 1), :], pattern=[[0, 1]], base=(32 * quad - SHIFT) % SEQ, channel_multiplier=1,
+        for b in range(BATCH):
+            nc.gpsimd.iota(pos[SEQ * b : SEQ * (b + 1), :], pattern=[[0, 1]], base=0, channel_multiplier=1,
                            allow_small_or_imprecise_dtypes=True)
         ratio = 10000.0 ** (-1.0 / PAIRS)
         freq = keep.tile([P, PAIRS], F32, name="freq")
@@ -129,83 +124,71 @@ def tile_selfattention_pa_kernel(tc, x_words, x_scales, w_qkv_words, w_qkv_scale
         nc.vector.tensor_copy(out=cos2[:], in_=trig[:, PAIRS : 2 * PAIRS].unsqueeze(2).to_broadcast([P, PAIRS, 2]))
         nsin = keep.tile([P, PAIRS], F32, name="nsin")
         nc.vector.tensor_scalar(out=nsin[:], in0=trig[:, 0:PAIRS], scalar1=-1.0, scalar2=None, op0=ALU.mult)
+
+        HB = N_TILE // HD
         cos_b = cos2[:].rearrange("p i e -> p (i e)").unsqueeze(1).to_broadcast([P, HB, HD])
         sin_b = trig[:, 0:PAIRS].unsqueeze(1).to_broadcast([P, HB, PAIRS])
         nsin_b = nsin[:].unsqueeze(1).to_broadcast([P, HB, PAIRS])
-        rotate(xs, xs_in, 1)
 
         acc = []
-        for j in range(BANKS):
+        for j in range(ALL_COLS // N_TILE):
             acc_j = psum.tile([P, N_TILE], F32, name="acc%d" % j)
             acc.append(acc_j)
 
-        def multiply(loads):
-            for first, n, j0, j1 in loads:
-                for g in range(first, first + n):
-                    for j in range(j0, j1):
-                        nc.tensor.matmul_mx(
-                            out=acc[j][:],
-                            lhsT=xw[:, g, :].bitcast(FP4X4),
-                            lhsT_scale=xs[:, g, :],
-                            rhs=codes[(g, j)].bitcast(FP4X4),
-                            rhs_scale=ws_of_pass[g][:, N_TILE * j : N_TILE * (j + 1)],
-                            start=(g == 0),
-                            stop=(g == PASSES - 1),
-                        )
+        def mm(j, g, codes):
+            nc.tensor.matmul_mx(
+                out=acc[j][:],
+                lhsT=xw[:, g, :].bitcast(FP4X4),
+                lhsT_scale=xs[:, g, :],
+                rhs=codes.bitcast(FP4X4),
+                rhs_scale=ws[ws_of_pass[g][0]][:, ws_of_pass[g][1], N_TILE * j : N_TILE * (j + 1)],
+                start=(g == 0),
+                stop=(g == PASSES - 1),
+            )
+
+        g = 0
+        for c, n in enumerate(QK_CHUNKS):
+            for i in range(n):
+                for j in range(QK_COLS // N_TILE):
+                    mm(j, g, wqk[c][:, i, 2 * N_TILE * j : 2 * N_TILE * (j + 1)])
+                g += 1
 
         res = []
         for t in range(3):
             res_t = keep.tile([P, HEADS * HD], F32, name="res%d" % t)
             res.append(res_t)
 
-        def store(eng, t, n0, n1, h0, h1):
-            b = n0 // SEQ
-            p0 = (n0 + SHIFT) % TOKENS
+        def store(eng, t, b):
             eng.dma_start(
-                out=outs[t][b, h0:h1, n0 - SEQ * b : n1 - SEQ * b, :].rearrange("h s d -> s h d"),
-                in_=res[t][p0 : p0 + n1 - n0, HD * h0 : HD * h1].rearrange("p (h d) -> p h d", d=HD),
+                out=outs[t][b].rearrange("h s d -> s h d"),
+                in_=res[t][SEQ * b : SEQ * (b + 1), :].rearrange("p (h d) -> p h d", h=HEADS),
             )
 
-        def rope_products(j):
+        for j in range(QK_COLS // N_TILE):
             u = acc[j][:].rearrange("p (h i e) -> p h i e", h=HB, e=2)
             cross = work.tile([P, 2, HB, PAIRS], F32, name="cross")
             nc.vector.tensor_tensor(out=cross[:, 0], in0=u[:, :, :, 1], in1=nsin_b, op=ALU.mult)
             nc.vector.tensor_tensor(out=cross[:, 1], in0=u[:, :, :, 0], in1=sin_b, op=ALU.mult)
             direct = work.tile([P, HB, HD], F32, name="direct")
             nc.vector.tensor_tensor(out=direct[:], in0=acc[j][:].rearrange("p (h d) -> p h d", h=HB), in1=cos_b, op=ALU.mult)
-            return direct, cross
-
-        def rope_sum(eng, j, direct, cross):
             half = N_TILE * (j % 2)
-            eng.tensor_tensor(
+            nc.gpsimd.tensor_tensor(
                 out=res[j // 2][:, half : half + N_TILE].rearrange("p (h i e) -> p h i e", h=HB, e=2),
                 in0=direct[:].rearrange("p h (i e) -> p h i e", e=2),
                 in1=cross[:].rearrange("p e h i -> p h i e"),
                 op=ALU.add,
             )
+            if j % 2 == 1:
+                store(nc.scalar, j // 2, 0)
+                store(nc.sync, j // 2, 1)
 
-        multiply(QK_LOADS)
-        for j in (0, 1):
-            direct, cross = rope_products(j)
-            rope_sum(nc.gpsimd, j, direct, cross)
-        store(nc.scalar, 0, 0, 64, 0, HEADS)
-        store(nc.gpsimd, 0, 64, 96, 0, HEADS)
-        store(nc.gpsimd, 0, 96, 128, 0, HEADS)
-        parts = []
-        for j in (2, 3):
-            parts.append(rope_products(j))
-        for j in (2, 3):
-            rope_sum(nc.vector, j, parts[j - 2][0], parts[j - 2][1])
-        store(nc.scalar, 1, 0, 64, 0, HEADS)
-        store(nc.sync, 1, 64, 96, 0, HEADS)
-        store(nc.sync, 1, 96, 128, 0, HEADS)
-        multiply(V0_LOADS)
+        g = 0
+        for c, n in enumerate(V_CHUNKS):
+            for i in range(n):
+                for j in range(V_COLS // N_TILE):
+                    mm(QK_COLS // N_TILE + j, g, wv[c][:, i, 2 * N_TILE * j : 2 * N_TILE * (j + 1)])
+                g += 1
         nc.scalar.copy(out=res[2][:, 0:N_TILE], in_=acc[4][:])
-        store(nc.scalar, 2, 0, 64, 0, HB)
-        store(nc.gpsimd, 2, 64, 96, 0, HB)
-        store(nc.gpsimd, 2, 96, 128, 0, HB)
-        multiply(V1_LOADS)
         nc.vector.tensor_copy(out=res[2][:, N_TILE : 2 * N_TILE], in_=acc[5][:])
-        store(nc.sync, 2, 0, 64, HB, HEADS)
-        store(nc.scalar, 2, 64, 96, HB, HEADS)
-        store(nc.scalar, 2, 96, 128, HB, HEADS)
+        store(nc.sync, 2, 0)
+        store(nc.scalar, 2, 1)

@@ -179,7 +179,7 @@ def tile_selfattention_pa_kernel(tc, x_words, x_scales, w_qkv_words, w_qkv_scale
                 op=ALU.add,
             )
             if j % 2 == 1:
-                store(nc.scalar, j // 2, 0)
+                store(nc.sync, j // 2, 0)
                 store(nc.sync, j // 2, 1)
 
         g = 0

@@ -38,6 +38,8 @@ def tile_selfattention_pa_kernel(tc, x_words, x_scales, w_qkv_words, w_qkv_scale
         psum = ctx.enter_context(tc.psum_pool(name="psum", bufs=1))
         ctx.enter_context(tc.manual_schedule())
 
+        xw_raw = keep.tile([P, PASSES, 2 * TOKENS], U8, name="xw_raw", align_bytes=64)
+        xs_raw = keep.tile([P, PASSES, TOKENS], U8, name="xs_raw", align_bytes=64)
         xw = keep.tile([P, PASSES, 2 * TOKENS], U8, name="xw", align_bytes=64)
         xs = keep.tile([P, PASSES, TOKENS], U8, name="xs", align_bytes=64)
         ws = []
@@ -56,7 +58,7 @@ def tile_selfattention_pa_kernel(tc, x_words, x_scales, w_qkv_words, w_qkv_scale
             wv_c = keep.tile([P, n, 2 * V_COLS], U8, name="wv%d" % c, align_bytes=64)
             wv.append(wv_c)
 
-        nc.vector.memset(xs[:].bitcast(I32), 0)
+        nc.vector.memset(xs_raw[:].bitcast(I32), 0)
         for k in range(len(SCALE_GROUPS)):
             nc.vector.memset(ws[k][:].bitcast(I32), 0)
 
@@ -77,23 +79,36 @@ def tile_selfattention_pa_kernel(tc, x_words, x_scales, w_qkv_words, w_qkv_scale
                 )
                 g0 += n
 
-        nc.sync.dma_start(out=xw[:].bitcast(I32), in_=x_words.rearrange("g p n -> p g n").bitcast(I32))
+        nc.sync.dma_start(out=xw_raw[:].bitcast(I32), in_=x_words.rearrange("g p n -> p g n").bitcast(I32))
+        for r in range(4):
+            nc.sync.dma_start(
+                out=xs_raw[r:P:32, :, :].bitcast(I32),
+                in_=x_scales[:, r:16:4, :].rearrange("g q n -> q g n").bitcast(I32),
+            )
         g0 = 0
         for k, n in enumerate(SCALE_GROUPS):
             load_scales(ws[k], w_qkv_scales[g0 : g0 + n])
             g0 += n
-        for r in range(4):
-            nc.sync.dma_start(
-                out=xs[r:P:32, :, :].bitcast(I32),
-                in_=x_scales[:, r:16:4, :].rearrange("g q n -> q g n").bitcast(I32),
-            )
         load_codes(wqk, QK_CHUNKS, 0, 2 * QK_COLS)
         load_codes(wv, V_CHUNKS, 2 * QK_COLS, 2 * ALL_COLS)
 
-        pos = keep.tile([P, 1], F32, name="pos")
         for b in range(BATCH):
-            nc.gpsimd.iota(pos[SEQ * b : SEQ * (b + 1), :], pattern=[[0, 1]], base=0, channel_multiplier=1,
-                           allow_small_or_imprecise_dtypes=True)
+            nc.vector.tensor_copy(
+                out=xw[:].rearrange("p g (s b e) -> p g s b e", b=BATCH, e=2)[:, :, :, b, :],
+                in_=xw_raw[:].rearrange("p g (b s e) -> p g b s e", b=BATCH, e=2)[:, :, b, :, :],
+            )
+        for b in range(BATCH):
+            nc.vector.tensor_copy(
+                out=xs[:].rearrange("p g (s b) -> p g s b", b=BATCH)[:, :, :, b],
+                in_=xs_raw[:].rearrange("p g (b s) -> p g b s", b=BATCH)[:, :, b, :],
+            )
+
+        part_i = keep.tile([P, 1], I32, name="part_i")
+        nc.gpsimd.iota(part_i[:], pattern=[[0, 1]], base=0, channel_multiplier=1)
+        pos_i = keep.tile([P, 1], I32, name="pos_i")
+        nc.vector.tensor_scalar(out=pos_i[:], in0=part_i[:], scalar1=1, scalar2=None, op0=ALU.arith_shift_right)
+        pos = keep.tile([P, 1], F32, name="pos")
+        nc.vector.tensor_copy(out=pos[:], in_=pos_i[:])
         ratio = 10000.0 ** (-1.0 / PAIRS)
         freq = keep.tile([P, PAIRS], F32, name="freq")
         nc.vector.memset(freq[:, 0:1], 1.0)
@@ -161,7 +176,7 @@ def tile_selfattention_pa_kernel(tc, x_words, x_scales, w_qkv_words, w_qkv_scale
         def store(eng, t, b):
             eng.dma_start(
                 out=outs[t][b].rearrange("h s d -> s h d"),
-                in_=res[t][SEQ * b : SEQ * (b + 1), :].rearrange("p (h d) -> p h d", h=HEADS),
+                in_=res[t][b:P:BATCH, :].rearrange("p (h d) -> p h d", h=HEADS),
             )
 
         for j in range(QK_COLS // N_TILE):

@@ -22,7 +22,7 @@ N_TILE = 512
 QK_COLS = 2048
 V_COLS = 1024
 ALL_COLS = QK_COLS + V_COLS
-SCALE_GROUPS = (4, 4, 8)
+SCALE_GROUPS = (4, 4, 6, 2)
 QK_CHUNKS = (1, 1, 2, 2, 2, 2, 2, 2, 2)
 V_CHUNKS = (4, 4, 4, 2, 1, 1)
 
@@ -86,9 +86,14 @@ def tile_selfattention_pa_kernel(tc, x_words, x_scales, w_qkv_words, w_qkv_scale
                 in_=x_scales[:, r:16:4, :].rearrange("g q n -> q g n").bitcast(I32),
             )
         g0 = 0
-        for k, n in enumerate(SCALE_GROUPS):
+        for k, n in enumerate(SCALE_GROUPS[:-1]):
             load_scales(ws[k], w_qkv_scales[g0 : g0 + n])
             g0 += n
+        for r in range(4):
+            nc.sync.dma_start(
+                out=ws[-1][r:P:32, :, :].bitcast(I32),
+                in_=w_qkv_scales[g0:PASSES, r:16:4, :].rearrange("g q n -> q g n").bitcast(I32),
+            )
         load_codes(wqk, QK_CHUNKS, 0, 2 * QK_COLS)
         load_codes(wv, V_CHUNKS, 2 * QK_COLS, 2 * ALL_COLS)
 

@@ -22,7 +22,7 @@ N_TILE = 512
 QK_COLS = 2048
 V_COLS = 1024
 ALL_COLS = QK_COLS + V_COLS
-SCALE_GROUPS = (4, 4, 6, 2)
+SCALE_GROUPS = (5, 8, 3)
 QK_CHUNKS = (1, 1, 2, 2, 2, 2, 2, 2, 2)
 V_CHUNKS = (4, 4, 4, 2, 1, 1)
 
@@ -86,14 +86,9 @@ def tile_selfattention_pa_kernel(tc, x_words, x_scales, w_qkv_words, w_qkv_scale
                 in_=x_scales[:, r:16:4, :].rearrange("g q n -> q g n").bitcast(I32),
             )
         g0 = 0
-        for k, n in enumerate(SCALE_GROUPS[:-1]):
+        for k, n in enumerate(SCALE_GROUPS):
             load_scales(ws[k], w_qkv_scales[g0 : g0 + n])
             g0 += n
-        for r in range(4):
-            nc.sync.dma_start(
-                out=ws[-1][r:P:32, :, :].bitcast(I32),
-                in_=w_qkv_scales[g0:PASSES, r:16:4, :].rearrange("g q n -> q g n").bitcast(I32),
-            )
         load_codes(wqk, QK_CHUNKS, 0, 2 * QK_COLS)
         load_codes(wv, V_CHUNKS, 2 * QK_COLS, 2 * ALL_COLS)
 

@@ -24,7 +24,7 @@ V_COLS = 1024
 ALL_COLS = QK_COLS + V_COLS
 SCALE_GROUPS = (5, 8, 3)
 QK_CHUNKS = (1, 1, 2, 2, 2, 2, 2, 2, 2)
-V_CHUNKS = (4, 4, 4, 2, 1, 1)
+V_CHUNKS = (3, 3, 2, 2, 2, 1, 1, 1, 1)
 
 FLOPS = 2 * TOKENS * 512 * PASSES * ALL_COLS
 

@@ -34,7 +34,7 @@ def tile_selfattention_pa_kernel(tc, x_words, x_scales, w_qkv_words, w_qkv_scale
     outs = (out_0, out_1, out_2)
     with ExitStack() as ctx:
         keep = ctx.enter_context(tc.tile_pool(name="keep", bufs=1))
-        work = ctx.enter_context(tc.tile_pool(name="work", bufs=2))
+        work = ctx.enter_context(tc.tile_pool(name="work", bufs=4))
         psum = ctx.enter_context(tc.psum_pool(name="psum", bufs=1))
         ctx.enter_context(tc.manual_schedule())
 
@@ -163,10 +163,13 @@ def tile_selfattention_pa_kernel(tc, x_words, x_scales, w_qkv_words, w_qkv_scale
 
         g = 0
         for c, n in enumerate(QK_CHUNKS):
-            for i in range(n):
-                for j in range(QK_COLS // N_TILE):
-                    mm(j, g, wqk[c][:, i, 2 * N_TILE * j : 2 * N_TILE * (j + 1)])
-                g += 1
+            if c < len(QK_CHUNKS) - 1:
+                order = [(i, j) for i in range(n) for j in range(QK_COLS // N_TILE)]
+            else:
+                order = [(i, j) for j in range(QK_COLS // N_TILE) for i in range(n)]
+            for i, j in order:
+                mm(j, g + i, wqk[c][:, i, 2 * N_TILE * j : 2 * N_TILE * (j + 1)])
+            g += n
 
         res = []
         for t in range(3):
@@ -187,7 +190,8 @@ def tile_selfattention_pa_kernel(tc, x_words, x_scales, w_qkv_words, w_qkv_scale
             direct = work.tile([P, HB, HD], F32, name="direct")
             nc.vector.tensor_tensor(out=direct[:], in0=acc[j][:].rearrange("p (h d) -> p h d", h=HB), in1=cos_b, op=ALU.mult)
             half = N_TILE * (j % 2)
-            nc.gpsimd.tensor_tensor(
+            add_engine = nc.gpsimd if j < QK_COLS // N_TILE - 1 else nc.vector
+            add_engine.tensor_tensor(
                 out=res[j // 2][:, half : half + N_TILE].rearrange("p (h i e) -> p h i e", h=HB, e=2),
                 in0=direct[:].rearrange("p h (i e) -> p h i e", e=2),
                 in1=cross[:].rearrange("p e h i -> p h i e"),

@@ -24,7 +24,8 @@ V_COLS = 1024
 ALL_COLS = QK_COLS + V_COLS
 SCALE_GROUPS = (5, 8, 3)
 QK_CHUNKS = (1, 1, 2, 2, 2, 2, 2, 2, 2)
-V_CHUNKS = (3, 3, 2, 2, 2, 1, 1, 1, 1)
+V_CHUNKS = (3, 3, 2, 2, 2, 1)
+V_END_CHUNKS = ((3,), (2, 1))
 
 FLOPS = 2 * TOKENS * 512 * PASSES * ALL_COLS
 
@@ -57,6 +58,12 @@ def tile_selfattention_pa_kernel(tc, x_words, x_scales, w_qkv_words, w_qkv_scale
         for c, n in enumerate(V_CHUNKS):
             wv_c = keep.tile([P, n, 2 * V_COLS], U8, name="wv%d" % c, align_bytes=64)
             wv.append(wv_c)
+        wv_end = []
+        for j, chunks in enumerate(V_END_CHUNKS):
+            wv_end.append([])
+            for c, n in enumerate(chunks):
+                wv_end_c = keep.tile([P, n, 2 * N_TILE], U8, name="wv_end%d_%d" % (j, c), align_bytes=64)
+                wv_end[j].append(wv_end_c)
 
         nc.vector.memset(xs_raw[:].bitcast(I32), 0)
         for k in range(len(SCALE_GROUPS)):
@@ -70,8 +77,7 @@ def tile_selfattention_pa_kernel(tc, x_words, x_scales, w_qkv_words, w_qkv_scale
                     in_=rows[:, q0:16:8, :].rearrange("g q n -> q g n").bitcast(I32),
                 )
 
-        def load_codes(tiles, chunks, col0, col1):
-            g0 = 0
+        def load_codes(tiles, chunks, col0, col1, g0=0):
             for c, n in enumerate(chunks):
                 nc.sync.dma_start(
                     out=tiles[c][:].bitcast(I32),
@@ -91,6 +97,8 @@ def tile_selfattention_pa_kernel(tc, x_words, x_scales, w_qkv_words, w_qkv_scale
             g0 += n
         load_codes(wqk, QK_CHUNKS, 0, 2 * QK_COLS)
         load_codes(wv, V_CHUNKS, 2 * QK_COLS, 2 * ALL_COLS)
+        for j, chunks in enumerate(V_END_CHUNKS):
+            load_codes(wv_end[j], chunks, 2 * (QK_COLS + N_TILE * j), 2 * (QK_COLS + N_TILE * (j + 1)), g0=sum(V_CHUNKS))
 
         for b in range(BATCH):
             nc.vector.tensor_copy(
@@ -172,9 +180,13 @@ def tile_selfattention_pa_kernel(tc, x_words, x_scales, w_qkv_words, w_qkv_scale
             g += n
 
         res = []
-        for t in range(3):
+        for t in range(2):
             res_t = keep.tile([P, HEADS * HD], F32, name="res%d" % t)
             res.append(res_t)
+        res_v = []
+        for j in range(V_COLS // N_TILE):
+            res_v_j = keep.tile([P, N_TILE], F32, name="res_v%d" % j)
+            res_v.append(res_v_j)
 
         def store(eng, t, b):
             eng.dma_start(
@@ -207,7 +219,22 @@ def tile_selfattention_pa_kernel(tc, x_words, x_scales, w_qkv_words, w_qkv_scale
                 for j in range(V_COLS // N_TILE):
                     mm(QK_COLS // N_TILE + j, g, wv[c][:, i, 2 * N_TILE * j : 2 * N_TILE * (j + 1)])
                 g += 1
-        nc.scalar.copy(out=res[2][:, 0:N_TILE], in_=acc[4][:])
-        nc.vector.tensor_copy(out=res[2][:, N_TILE : 2 * N_TILE], in_=acc[5][:])
-        store(nc.sync, 2, 0)
-        store(nc.scalar, 2, 1)
+
+        def store_v(eng, j, b):
+            eng.dma_start(
+                out=outs[2][b, HB * j : HB * (j + 1)].rearrange("h s d -> s h d"),
+                in_=res_v[j][b:P:BATCH, :].rearrange("p (h d) -> p h d", h=HB),
+            )
+
+        for j, chunks in enumerate(V_END_CHUNKS):
+            g = sum(V_CHUNKS)
+            for c, n in enumerate(chunks):
+                for i in range(n):
+                    mm(QK_COLS // N_TILE + j, g, wv_end[j][c][:, i, :])
+                    g += 1
+            if j == 0:
+                nc.scalar.copy(out=res_v[j][:], in_=acc[QK_COLS // N_TILE + j][:])
+            else:
+                nc.vector.tensor_copy(out=res_v[j][:], in_=acc[QK_COLS // N_TILE + j][:])
+            store_v(nc.sync, j, 0)
+            store_v(nc.scalar, j, 1)

@@ -39,30 +39,30 @@ def tile_selfattention_pa_kernel(tc, x_words, x_scales, w_qkv_words, w_qkv_scale
         psum = ctx.enter_context(tc.psum_pool(name="psum", bufs=1))
         ctx.enter_context(tc.manual_schedule())
 
-        xw_raw = keep.tile([P, PASSES, 2 * TOKENS], U8, name="xw_raw", align_bytes=64)
-        xs_raw = keep.tile([P, PASSES, TOKENS], U8, name="xs_raw", align_bytes=64)
-        xw = keep.tile([P, PASSES, 2 * TOKENS], U8, name="xw", align_bytes=64)
-        xs = keep.tile([P, PASSES, TOKENS], U8, name="xs", align_bytes=64)
+        xw_raw = keep.tile([P, PASSES, 2 * TOKENS], U8, name="xw_raw", align_bytes=256)
+        xs_raw = keep.tile([P, PASSES, TOKENS], U8, name="xs_raw", align_bytes=256)
+        xw = keep.tile([P, PASSES, 2 * TOKENS], U8, name="xw", align_bytes=256)
+        xs = keep.tile([P, PASSES, TOKENS], U8, name="xs", align_bytes=256)
         ws = []
         ws_of_pass = []
         for k, n in enumerate(SCALE_GROUPS):
-            ws_k = keep.tile([P, n, ALL_COLS], U8, name="ws%d" % k, align_bytes=64)
+            ws_k = keep.tile([P, n, ALL_COLS], U8, name="ws%d" % k, align_bytes=256)
             ws.append(ws_k)
             for i in range(n):
                 ws_of_pass.append((k, i))
         wqk = []
         for c, n in enumerate(QK_CHUNKS):
-            wqk_c = keep.tile([P, n, 2 * QK_COLS], U8, name="wqk%d" % c, align_bytes=64)
+            wqk_c = keep.tile([P, n, 2 * QK_COLS], U8, name="wqk%d" % c, align_bytes=256)
             wqk.append(wqk_c)
         wv = []
         for c, n in enumerate(V_CHUNKS):
-            wv_c = keep.tile([P, n, 2 * V_COLS], U8, name="wv%d" % c, align_bytes=64)
+            wv_c = keep.tile([P, n, 2 * V_COLS], U8, name="wv%d" % c, align_bytes=256)
             wv.append(wv_c)
         wv_end = []
         for j, chunks in enumerate(V_END_CHUNKS):
             wv_end.append([])
             for c, n in enumerate(chunks):
-                wv_end_c = keep.tile([P, n, 2 * N_TILE], U8, name="wv_end%d_%d" % (j, c), align_bytes=64)
+                wv_end_c = keep.tile([P, n, 2 * N_TILE], U8, name="wv_end%d_%d" % (j, c), align_bytes=256)
                 wv_end[j].append(wv_end_c)
 
         nc.vector.memset(xs_raw[:].bitcast(I32), 0)
@@ -181,11 +181,11 @@ def tile_selfattention_pa_kernel(tc, x_words, x_scales, w_qkv_words, w_qkv_scale
 
         res = []
         for t in range(2):
-            res_t = keep.tile([P, HEADS * HD], F32, name="res%d" % t)
+            res_t = keep.tile([P, HEADS * HD], F32, name="res%d" % t, align_bytes=256)
             res.append(res_t)
         res_v = []
         for j in range(V_COLS // N_TILE):
-            res_v_j = keep.tile([P, N_TILE], F32, name="res_v%d" % j)
+            res_v_j = keep.tile([P, N_TILE], F32, name="res_v%d" % j, align_bytes=256)
             res_v.append(res_v_j)
 
         def store(eng, t, b):

import math
from contextlib import ExitStack

import concourse.mybir as mybir

F32 = mybir.dt.float32
I32 = mybir.dt.int32
U8 = mybir.dt.uint8
FP4X4 = mybir.dt.float4_e2m1fn_x4
ALU = mybir.AluOpType
ACT = mybir.ActivationFunctionType

P = 128
PASSES = 16
TOKENS = 128
BATCH = 2
SEQ = 64
HEADS = 8
HD = 128
PAIRS = HD // 2
N_TILE = 512
QK_COLS = 2048
V_COLS = 1024
ALL_COLS = QK_COLS + V_COLS
SCALE_GROUPS = (5, 8, 3)
QK_CHUNKS = (1, 1, 2, 2, 2, 2, 2, 2, 2)
V_CHUNKS = (3, 3, 2, 2, 2, 1)
V_END_CHUNKS = ((3,), (2, 1))

FLOPS = 2 * TOKENS * 512 * PASSES * ALL_COLS


def tile_selfattention_pa_kernel(tc, x_words, x_scales, w_qkv_words, w_qkv_scales, out_0, out_1, out_2):
    nc = tc.nc
    outs = (out_0, out_1, out_2)
    with ExitStack() as ctx:
        keep = ctx.enter_context(tc.tile_pool(name="keep", bufs=1))
        work = ctx.enter_context(tc.tile_pool(name="work", bufs=4))
        psum = ctx.enter_context(tc.psum_pool(name="psum", bufs=1))
        ctx.enter_context(tc.manual_schedule())

        xw_raw = keep.tile([P, PASSES, 2 * TOKENS], U8, name="xw_raw", align_bytes=256)
        xs_raw = keep.tile([P, PASSES, TOKENS], U8, name="xs_raw", align_bytes=256)
        xw = keep.tile([P, PASSES, 2 * TOKENS], U8, name="xw", align_bytes=256)
        xs = keep.tile([P, PASSES, TOKENS], U8, name="xs", align_bytes=256)
        ws = []
        ws_of_pass = []
        for k, n in enumerate(SCALE_GROUPS):
            ws_k = keep.tile([P, n, ALL_COLS], U8, name="ws%d" % k, align_bytes=256)
            ws.append(ws_k)
            for i in range(n):
                ws_of_pass.append((k, i))
        wqk = []
        for c, n in enumerate(QK_CHUNKS):
            wqk_c = keep.tile([P, n, 2 * QK_COLS], U8, name="wqk%d" % c, align_bytes=256)
            wqk.append(wqk_c)
        wv = []
        for c, n in enumerate(V_CHUNKS):
            wv_c = keep.tile([P, n, 2 * V_COLS], U8, name="wv%d" % c, align_bytes=256)
            wv.append(wv_c)
        wv_end = []
        for j, chunks in enumerate(V_END_CHUNKS):
            wv_end.append([])
            for c, n in enumerate(chunks):
                wv_end_c = keep.tile([P, n, 2 * N_TILE], U8, name="wv_end%d_%d" % (j, c), align_bytes=256)
                wv_end[j].append(wv_end_c)

        nc.vector.memset(xs_raw[:].bitcast(I32), 0)
        for k in range(len(SCALE_GROUPS)):
            nc.vector.memset(ws[k][:].bitcast(I32), 0)

        def load_scales(plane, rows):
            for q0 in range(8):
                p0 = 32 * (q0 // 4) + q0 % 4
                nc.sync.dma_start(
                    out=plane[p0:P:64, :, :].bitcast(I32),
                    in_=rows[:, q0:16:8, :].rearrange("g q n -> q g n").bitcast(I32),
                )

        def load_codes(tiles, chunks, col0, col1, g0=0):
            for c, n in enumerate(chunks):
                nc.sync.dma_start(
                    out=tiles[c][:].bitcast(I32),
                    in_=w_qkv_words[g0 : g0 + n, :, col0:col1].rearrange("g p n -> p g n").bitcast(I32),
                )
                g0 += n

        nc.sync.dma_start(out=xw_raw[:].bitcast(I32), in_=x_words.rearrange("g p n -> p g n").bitcast(I32))
        for r in range(4):
            nc.sync.dma_start(
                out=xs_raw[r:P:32, :, :].bitcast(I32),
                in_=x_scales[:, r:16:4, :].rearrange("g q n -> q g n").bitcast(I32),
            )
        g0 = 0
        for k, n in enumerate(SCALE_GROUPS):
            load_scales(ws[k], w_qkv_scales[g0 : g0 + n])
            g0 += n
        load_codes(wqk, QK_CHUNKS, 0, 2 * QK_COLS)
        load_codes(wv, V_CHUNKS, 2 * QK_COLS, 2 * ALL_COLS)
        for j, chunks in enumerate(V_END_CHUNKS):
            load_codes(wv_end[j], chunks, 2 * (QK_COLS + N_TILE * j), 2 * (QK_COLS + N_TILE * (j + 1)), g0=sum(V_CHUNKS))

        for b in range(BATCH):
            nc.vector.tensor_copy(
                out=xw[:].rearrange("p g (s b e) -> p g s b e", b=BATCH, e=2)[:, :, :, b, :],
                in_=xw_raw[:].rearrange("p g (b s e) -> p g b s e", b=BATCH, e=2)[:, :, b, :, :],
            )
        for b in range(BATCH):
            nc.vector.tensor_copy(
                out=xs[:].rearrange("p g (s b) -> p g s b", b=BATCH)[:, :, :, b],
                in_=xs_raw[:].rearrange("p g (b s) -> p g b s", b=BATCH)[:, :, b, :],
            )

        part_i = keep.tile([P, 1], I32, name="part_i")
        nc.gpsimd.iota(part_i[:], pattern=[[0, 1]], base=0, channel_multiplier=1)
        pos_i = keep.tile([P, 1], I32, name="pos_i")
        nc.vector.tensor_scalar(out=pos_i[:], in0=part_i[:], scalar1=1, scalar2=None, op0=ALU.arith_shift_right)
        pos = keep.tile([P, 1], F32, name="pos")
        nc.vector.tensor_copy(out=pos[:], in_=pos_i[:])
        ratio = 10000.0 ** (-1.0 / PAIRS)
        freq = keep.tile([P, PAIRS], F32, name="freq")
        nc.vector.memset(freq[:, 0:1], 1.0)
        for s in range(6):
            w = 2 ** s
            nc.vector.tensor_scalar(out=freq[:, w : 2 * w], in0=freq[:, 0:w], scalar1=ratio ** w, scalar2=None, op0=ALU.mult)
        ang = keep.tile([P, 2 * PAIRS], F32, name="ang")
        nc.vector.tensor_scalar(out=ang[:, 0:PAIRS], in0=freq[:], scalar1=pos[:, 0:1], scalar2=None, op0=ALU.mult)
        nc.vector.tensor_scalar(out=ang[:, PAIRS : 2 * PAIRS], in0=freq[:], scalar1=pos[:, 0:1], scalar2=math.pi / 2,
                                op0=ALU.mult, op1=ALU.add)
        turns_i = keep.tile([P, 2 * PAIRS], I32, name="turns_i")
        nc.vector.tensor_scalar(out=turns_i[:], in0=ang[:], scalar1=1.0 / (2.0 * math.pi), scalar2=None, op0=ALU.mult)
        turns_f = keep.tile([P, 2 * PAIRS], F32, name="turns_f")
        nc.vector.tensor_copy(out=turns_f[:], in_=turns_i[:])
        red0 = keep.tile([P, 2 * PAIRS], F32, name="red0")
        nc.vector.scalar_tensor_tensor(out=red0[:], in0=turns_f[:], scalar=-2.0 * math.pi, in1=ang[:], op0=ALU.mult, op1=ALU.add)
        fix0 = keep.tile([P, 2 * PAIRS], F32, name="fix0")
        nc.vector.tensor_scalar(out=fix0[:], in0=red0[:], scalar1=math.pi, scalar2=-2.0 * math.pi, op0=ALU.is_gt, op1=ALU.mult)
        red1 = keep.tile([P, 2 * PAIRS], F32, name="red1")
        nc.vector.tensor_tensor(out=red1[:], in0=red0[:], in1=fix0[:], op=ALU.add)
        fix1 = keep.tile([P, 2 * PAIRS], F32, name="fix1")
        nc.vector.tensor_scalar(out=fix1[:], in0=red1[:], scalar1=-math.pi, scalar2=2.0 * math.pi, op0=ALU.is_lt, op1=ALU.mult)
        red2 = keep.tile([P, 2 * PAIRS], F32, name="red2")
        nc.vector.tensor_tensor(out=red2[:], in0=red1[:], in1=fix1[:], op=ALU.add)
        trig = keep.tile([P, 2 * PAIRS], F32, name="trig")
        nc.scalar.activation(out=trig[:], in_=red2[:], func=ACT.Sin)
        cos2 = keep.tile([P, PAIRS, 2], F32, name="cos2")
        nc.vector.tensor_copy(out=cos2[:], in_=trig[:, PAIRS : 2 * PAIRS].unsqueeze(2).to_broadcast([P, PAIRS, 2]))
        nsin = keep.tile([P, PAIRS], F32, name="nsin")
        nc.vector.tensor_scalar(out=nsin[:], in0=trig[:, 0:PAIRS], scalar1=-1.0, scalar2=None, op0=ALU.mult)

        HB = N_TILE // HD
        cos_b = cos2[:].rearrange("p i e -> p (i e)").unsqueeze(1).to_broadcast([P, HB, HD])
        sin_b = trig[:, 0:PAIRS].unsqueeze(1).to_broadcast([P, HB, PAIRS])
        nsin_b = nsin[:].unsqueeze(1).to_broadcast([P, HB, PAIRS])

        acc = []
        for j in range(ALL_COLS // N_TILE):
            acc_j = psum.tile([P, N_TILE], F32, name="acc%d" % j)
            acc.append(acc_j)

        def mm(j, g, codes):
            nc.tensor.matmul_mx(
                out=acc[j][:],
                lhsT=xw[:, g, :].bitcast(FP4X4),
                lhsT_scale=xs[:, g, :],
                rhs=codes.bitcast(FP4X4),
                rhs_scale=ws[ws_of_pass[g][0]][:, ws_of_pass[g][1], N_TILE * j : N_TILE * (j + 1)],
                start=(g == 0),
                stop=(g == PASSES - 1),
            )

        g = 0
        for c, n in enumerate(QK_CHUNKS):
            if c < len(QK_CHUNKS) - 1:
                order = [(i, j) for i in range(n) for j in range(QK_COLS // N_TILE)]
            else:
                order = [(i, j) for j in range(QK_COLS // N_TILE) for i in range(n)]
            for i, j in order:
                mm(j, g + i, wqk[c][:, i, 2 * N_TILE * j : 2 * N_TILE * (j + 1)])
            g += n

        res = []
        for t in range(2):
            res_t = keep.tile([P, HEADS * HD], F32, name="res%d" % t, align_bytes=256)
            res.append(res_t)
        res_v = []
        for j in range(V_COLS // N_TILE):
            res_v_j = keep.tile([P, N_TILE], F32, name="res_v%d" % j, align_bytes=256)
            res_v.append(res_v_j)

        def store(eng, t, b):
            eng.dma_start(
                out=outs[t][b].rearrange("h s d -> s h d"),
                in_=res[t][b:P:BATCH, :].rearrange("p (h d) -> p h d", h=HEADS),
            )

        for j in range(QK_COLS // N_TILE):
            u = acc[j][:].rearrange("p (h i e) -> p h i e", h=HB, e=2)
            cross = work.tile([P, 2, HB, PAIRS], F32, name="cross")
            nc.vector.tensor_tensor(out=cross[:, 0], in0=u[:, :, :, 1], in1=nsin_b, op=ALU.mult)
            nc.vector.tensor_tensor(out=cross[:, 1], in0=u[:, :, :, 0], in1=sin_b, op=ALU.mult)
            direct = work.tile([P, HB, HD], F32, name="direct")
            nc.vector.tensor_tensor(out=direct[:], in0=acc[j][:].rearrange("p (h d) -> p h d", h=HB), in1=cos_b, op=ALU.mult)
            half = N_TILE * (j % 2)
            add_engine = nc.gpsimd if j < QK_COLS // N_TILE - 1 else nc.vector
            add_engine.tensor_tensor(
                out=res[j // 2][:, half : half + N_TILE].rearrange("p (h i e) -> p h i e", h=HB, e=2),
                in0=direct[:].rearrange("p h (i e) -> p h i e", e=2),
                in1=cross[:].rearrange("p e h i -> p h i e"),
                op=ALU.add,
            )
            if j % 2 == 1:
                store(nc.sync, j // 2, 0)
                store(nc.sync, j // 2, 1)

        g = 0
        for c, n in enumerate(V_CHUNKS):
            for i in range(n):
                for j in range(V_COLS // N_TILE):
                    mm(QK_COLS // N_TILE + j, g, wv[c][:, i, 2 * N_TILE * j : 2 * N_TILE * (j + 1)])
                g += 1

        def store_v(eng, j, b):
            eng.dma_start(
                out=outs[2][b, HB * j : HB * (j + 1)].rearrange("h s d -> s h d"),
                in_=res_v[j][b:P:BATCH, :].rearrange("p (h d) -> p h d", h=HB),
            )

        for j, chunks in enumerate(V_END_CHUNKS):
            g = sum(V_CHUNKS)
            for c, n in enumerate(chunks):
                for i in range(n):
                    mm(QK_COLS // N_TILE + j, g, wv_end[j][c][:, i, :])
                    g += 1
            if j == 0:
                nc.scalar.copy(out=res_v[j][:], in_=acc[QK_COLS // N_TILE + j][:])
            else:
                nc.vector.tensor_copy(out=res_v[j][:], in_=acc[QK_COLS // N_TILE + j][:])
            store_v(nc.sync, j, 0)
            store_v(nc.scalar, j, 1)
